import numpy as np
import ml_dtypes


def mxq(x, axis, fmt="e4m3"):
    dtype, down = {"e4m3": (ml_dtypes.float8_e4m3fn, 7), "e5m2": (ml_dtypes.float8_e5m2, 14)}[fmt]
    v = np.moveaxis(np.asarray(x, np.float32).astype(ml_dtypes.bfloat16).astype(np.float64), axis, -1)
    blocks = v.reshape(v.shape[:-1] + (-1, 32))
    amax = np.abs(blocks).max(-1, keepdims=True)
    byte = np.maximum(np.where(amax > 0, np.frexp(amax)[1] - 1 + 127, 0) - down, 1)
    scale = np.exp2(byte - 127.0)
    codes = (blocks / scale).astype(np.float32).astype(dtype).astype(np.float64)
    return np.moveaxis((codes * scale).reshape(v.shape), -1, axis)


WIDE = False


def mx_kscale(k):
    if not WIDE:
        return np.ones(k)
    levels = np.array([20, -20, 10, -10, 0])
    a = np.random.permutation(np.resize(levels, k // 512 * 4)).reshape(k // 512, 4)
    idx = np.arange(k)
    return np.exp2(a[idx // 512, idx % 128 // 32])


BF16 = ml_dtypes.bfloat16


def bf(x):
    return np.asarray(x, np.float32).astype(BF16)


def f64(x):
    return np.asarray(x).astype(np.float64)


I, H, B = 1536, 1536, 512


def sigmoid(v):
    return 1.0 / (1.0 + np.exp(-v))


def setup_inputs():
    u = mx_kscale(H)[:, None]
    x = bf(np.random.standard_normal((I, B)))
    h = bf(np.random.standard_normal((B, H)))
    w_ii0 = bf(np.random.standard_normal((H, I)) * 0.7 / np.sqrt(I))
    w_ig0 = bf(np.random.standard_normal((H, I)) * 0.7 / np.sqrt(I))
    w_hi = bf(np.random.standard_normal((H, H)) * 0.7 / np.sqrt(H))
    w_hg = bf(np.random.standard_normal((H, H)) * 0.7 / np.sqrt(H))
    b_ii = bf(np.random.standard_normal((H, 1)) * 0.3)
    b_hi = bf(np.random.standard_normal((H, 1)) * 0.3)
    b_ig = bf(np.random.standard_normal((H, 1)) * 0.3)
    b_hg = bf(np.random.standard_normal((H, 1)) * 0.3)
    g = bf(np.random.standard_normal((H, B)) * np.exp2(np.random.randint(-12, 1, (1, B))) * 64.0 * u)
    gi = sigmoid(f64(w_ii0) @ f64(x) + f64(b_ii) + f64(w_hi) @ f64(h).T + f64(b_hi))
    cg = np.tanh(f64(w_ig0) @ f64(x) + f64(b_ig) + f64(w_hg) @ f64(h).T + f64(b_hg))
    return {"x": x, "h": h, "w_ii": bf(f64(w_ii0) / u), "w_ig": bf(f64(w_ig0) / u), "w_hi": w_hi, "w_hg": w_hg,
            "b_ii": b_ii, "b_hi": b_hi, "b_ig": b_ig, "b_hg": b_hg,
            "gate_i": np.asarray(gi, np.float32), "cand_g": np.asarray(cg, np.float32), "grad_out": g}


def reference(x, h, w_ii, w_ig, w_hi, w_hg, b_ii, b_hi, b_ig, b_hg, gate_i, cand_g, grad_out):
    go = f64(grad_out)
    i = f64(gate_i)
    g = f64(cand_g)
    dzi = go * g * i * (1.0 - i)
    dzg = go * i * (1.0 - g * g)
    a = mxq(f64(w_ii), 0, "e4m3").T @ mxq(dzi, 0, "e5m2")
    c = mxq(f64(w_ig), 0, "e4m3").T @ mxq(dzg, 0, "e5m2")
    return a + c

@@ -1,0 +1,175 @@
+from contextlib import ExitStack
+
+import concourse.mybir as mybir
+
+F32 = mybir.dt.float32
+BF16 = mybir.dt.bfloat16
+U32 = mybir.dt.uint32
+U8 = mybir.dt.uint8
+E4M3_X4 = mybir.dt.float8_e4m3fn_x4
+E5M2_X4 = mybir.dt.float8_e5m2_x4
+MULT = mybir.AluOpType.mult
+SUBTRACT = mybir.AluOpType.subtract
+SQUARE = mybir.ActivationFunctionType.Square
+
+P = 128
+PACK = 4
+K_PASS = P * PACK
+HIDDEN = 1536
+FEATURES = 1536
+BATCH = 512
+CHUNKS = HIDDEN // K_PASS
+PIECE = 512
+TILES_IN_PIECE = PIECE // P
+PSUM_BANKS = 8
+RUN = 4
+
+PATHS = 2
+CANDIDATE = 0
+INPUT_GATE = 1
+
+FIRST_ROUND_PIECES = (0, 1)
+SECOND_ROUND_PIECES = (2,)
+
+FLOPS = 2 * PATHS * HIDDEN * FEATURES * BATCH
+BYTES = PATHS * HIDDEN * FEATURES * 2 + 2 * HIDDEN * BATCH * 4 + HIDDEN * BATCH * 2 + FEATURES * BATCH * 4
+
+
+def rows_to_partitions(dram, c):
+    return dram[c * K_PASS : (c + 1) * K_PASS, :].rearrange("(p j) w -> p j w", j=PACK)
+
+
+def by_row(tile_view):
+    return tile_view.rearrange("p j (c r) -> p c j r", r=RUN)
+
+
+def by_column(tile_view):
+    return tile_view.rearrange("p (c r) j -> p c j r", r=RUN)
+
+
+def tile_naivelstm_pa_v_kernel(
+    tc, x, h, w_ii, w_ig, w_hi, w_hg, b_ii, b_hi, b_ig, b_hg, gate_i, cand_g, grad_out, out
+):
+    nc = tc.nc
+    weights = {CANDIDATE: w_ig, INPUT_GATE: w_ii}
+
+    with ExitStack() as pools:
+        resident = pools.enter_context(tc.tile_pool(name="resident", bufs=1))
+        saved = pools.enter_context(tc.tile_pool(name="saved", bufs=2))
+        scratch = pools.enter_context(tc.tile_pool(name="scratch", bufs=1))
+        grouped = pools.enter_context(tc.tile_pool(name="grouped", bufs=1))
+        results = pools.enter_context(tc.tile_pool(name="results", bufs=3))
+        banks = pools.enter_context(tc.psum_pool(name="banks", bufs=PSUM_BANKS))
+
+        w_codes = resident.tile([P, PATHS, CHUNKS, FEATURES], U32, align_bytes=64)
+        w_scales = resident.tile([P, PATHS, CHUNKS, FEATURES], U8, align_bytes=64)
+        dz_codes = resident.tile([P, PATHS, CHUNKS, BATCH], U32, align_bytes=64)
+        dz_scales = resident.tile([P, PATHS, CHUNKS, BATCH], U8, align_bytes=64)
+
+        w_raw = {}
+        chunk_inputs = {}
+
+        def load_chunk(c):
+            grad = saved.tile([P, PACK, BATCH], BF16, name="grad")
+            gate = saved.tile([P, PACK, BATCH], F32, name="gate")
+            cand = saved.tile([P, PACK, BATCH], F32, name="cand")
+            nc.sync.dma_start(out=grad[:], in_=rows_to_partitions(grad_out, c))
+            nc.sync.dma_start(out=gate[:], in_=rows_to_partitions(gate_i, c))
+            nc.sync.dma_start(out=cand[:], in_=rows_to_partitions(cand_g, c))
+            chunk_inputs[c] = (grad, gate, cand)
+            for path in (CANDIDATE, INPUT_GATE):
+                w_raw[path, c] = resident.tile([P, PACK, FEATURES], BF16, name="w_raw_%d_%d" % (path, c))
+                nc.sync.dma_start(out=w_raw[path, c][:], in_=rows_to_partitions(weights[path], c))
+
+        def quantise_weights(path, c, piece, copy, tag, bufs):
+            cols = slice(piece * PIECE, (piece + 1) * PIECE)
+            w_grouped = grouped.tile([P, PIECE, PACK], BF16, name=tag, bufs=bufs, align_bytes=64)
+            copy(out=by_column(w_grouped[:]), in_=by_row(w_raw[path, c][:, :, cols]))
+            nc.vector.quantize_mx(
+                out=w_codes[:, path, c, cols].bitcast(E4M3_X4),
+                scales=w_scales[:, path, c, cols],
+                in_=w_grouped[:].rearrange("p w j -> p (w j)"),
+            )
+
+        def quantise_dz(path, c, dz_grouped):
+            nc.vector.quantize_mx(
+                out=dz_codes[:, path, c, :].bitcast(E5M2_X4),
+                scales=dz_scales[:, path, c, :],
+                in_=dz_grouped[:].rearrange("p w j -> p (w j)"),
+            )
+
+        def multiply(path, c, pieces, sums):
+            for piece in pieces:
+                for t in range(piece * TILES_IN_PIECE, (piece + 1) * TILES_IN_PIECE):
+                    cols = slice(t * P, (t + 1) * P)
+                    nc.tensor.matmul_mx(
+                        out=sums[t][:],
+                        lhsT=w_codes[:, path, c, cols].bitcast(E4M3_X4),
+                        lhsT_scale=w_scales[:, path, c, cols],
+                        rhs=dz_codes[:, path, c, :].bitcast(E5M2_X4),
+                        rhs_scale=dz_scales[:, path, c, :],
+                        start=(c == 0 and path == CANDIDATE),
+                        stop=(c == CHUNKS - 1 and path == INPUT_GATE),
+                    )
+
+        def open_sums(pieces):
+            sums = {}
+            for piece in pieces:
+                for t in range(piece * TILES_IN_PIECE, (piece + 1) * TILES_IN_PIECE):
+                    sums[t] = banks.tile([P, BATCH], F32, name="sum")
+            return sums
+
+        def store_sums(sums):
+            for t in sorted(sums):
+                result = results.tile([P, BATCH], F32, name="result")
+                if t % 2 == 0:
+                    nc.scalar.copy(out=result[:], in_=sums[t][:])
+                else:
+                    nc.vector.tensor_copy(out=result[:], in_=sums[t][:])
+                nc.sync.dma_start(out=out[t * P : (t + 1) * P, :], in_=result[:])
+
+        sums = open_sums(FIRST_ROUND_PIECES)
+        load_chunk(0)
+        for c in range(CHUNKS):
+            if c + 1 < CHUNKS:
+                load_chunk(c + 1)
+            grad, gate, cand = chunk_inputs[c]
+
+            cand_sq = scratch.tile([P, PACK, BATCH], F32, name="cand_sq", bufs=2)
+            nc.scalar.activation(out=cand_sq[:], in_=cand[:], func=SQUARE)
+            neg_gi = scratch.tile([P, PACK, BATCH], F32, name="neg_gi")
+            nc.vector.scalar_tensor_tensor(
+                out=neg_gi[:], in0=gate[:], scalar=-1.0, in1=grad[:], op0=MULT, op1=MULT
+            )
+            nc.vector.scalar_tensor_tensor(
+                out=gate[:], in0=gate[:], scalar=1.0, in1=cand[:], op0=SUBTRACT, op1=MULT
+            )
+            dzg = grouped.tile([P, BATCH, PACK], BF16, name="dzg", align_bytes=64)
+            nc.vector.scalar_tensor_tensor(
+                out=dzg[:],
+                in0=cand_sq[:].rearrange("p j w -> p w j"),
+                scalar=1.0,
+                in1=neg_gi[:].rearrange("p j w -> p w j"),
+                op0=SUBTRACT,
+                op1=MULT,
+            )
+            for piece in FIRST_ROUND_PIECES:
+                quantise_weights(CANDIDATE, c, piece, nc.scalar.copy, "w_first", 3)
+            quantise_dz(CANDIDATE, c, dzg)
+            dzi = grouped.tile([P, BATCH, PACK], BF16, name="dzi", align_bytes=64)
+            nc.vector.tensor_tensor(out=by_column(dzi[:]), in0=by_row(neg_gi[:]), in1=by_row(gate[:]), op=MULT)
+            multiply(CANDIDATE, c, FIRST_ROUND_PIECES, sums)
+            for piece in FIRST_ROUND_PIECES:
+                quantise_weights(INPUT_GATE, c, piece, nc.scalar.copy, "w_first", 3)
+            quantise_dz(INPUT_GATE, c, dzi)
+            multiply(INPUT_GATE, c, FIRST_ROUND_PIECES, sums)
+        store_sums(sums)
+
+        sums = open_sums(SECOND_ROUND_PIECES)
+        for c in range(CHUNKS):
+            for piece in SECOND_ROUND_PIECES:
+                quantise_weights(CANDIDATE, c, piece, nc.scalar.copy, "w_second", 2)
+                quantise_weights(INPUT_GATE, c, piece, nc.vector.tensor_copy, "w_second", 2)
+            multiply(CANDIDATE, c, SECOND_ROUND_PIECES, sums)
+            multiply(INPUT_GATE, c, SECOND_ROUND_PIECES, sums)
+        store_sums(sums)

@@ -23,13 +23,16 @@ PIECE = 512
 TILES_IN_PIECE = PIECE // P
 PSUM_BANKS = 8
 RUN = 4
+HALVES = 2
+ROWS_IN_HALF = PACK // HALVES
+CHUNKS_AHEAD = 2
 
 PATHS = 2
 CANDIDATE = 0
 INPUT_GATE = 1
 
 FIRST_ROUND_PIECES = (0, 1)
-SECOND_ROUND_PIECES = (2,)
+SECOND_ROUND_PIECE = 2
 
 FLOPS = 2 * PATHS * HIDDEN * FEATURES * BATCH
 BYTES = PATHS * HIDDEN * FEATURES * 2 + 2 * HIDDEN * BATCH * 4 + HIDDEN * BATCH * 2 + FEATURES * BATCH * 4
@@ -47,103 +50,138 @@ def by_column(tile_view):
     return tile_view.rearrange("p (c r) j -> p c j r", r=RUN)
 
 
+def tiles_of(piece):
+    return range(piece * TILES_IN_PIECE, (piece + 1) * TILES_IN_PIECE)
+
+
 def tile_naivelstm_pa_v_kernel(
     tc, x, h, w_ii, w_ig, w_hi, w_hg, b_ii, b_hi, b_ig, b_hg, gate_i, cand_g, grad_out, out
 ):
     nc = tc.nc
     weights = {CANDIDATE: w_ig, INPUT_GATE: w_ii}
 
-    with ExitStack() as pools:
-        resident = pools.enter_context(tc.tile_pool(name="resident", bufs=1))
-        saved = pools.enter_context(tc.tile_pool(name="saved", bufs=2))
-        scratch = pools.enter_context(tc.tile_pool(name="scratch", bufs=1))
-        grouped = pools.enter_context(tc.tile_pool(name="grouped", bufs=1))
-        results = pools.enter_context(tc.tile_pool(name="results", bufs=3))
-        banks = pools.enter_context(tc.psum_pool(name="banks", bufs=PSUM_BANKS))
+    with ExitStack() as stack:
+        resident = stack.enter_context(tc.tile_pool(name="resident", bufs=1))
+        saved = stack.enter_context(tc.tile_pool(name="saved", bufs=CHUNKS_AHEAD))
+        scratch = stack.enter_context(tc.tile_pool(name="scratch", bufs=1))
+        grouped = stack.enter_context(tc.tile_pool(name="grouped", bufs=1))
+        results = stack.enter_context(tc.tile_pool(name="results", bufs=PSUM_BANKS))
+        banks = stack.enter_context(tc.psum_pool(name="banks", bufs=PSUM_BANKS))
+        stack.enter_context(tc.manual_schedule())
 
         w_codes = resident.tile([P, PATHS, CHUNKS, FEATURES], U32, align_bytes=64)
         w_scales = resident.tile([P, PATHS, CHUNKS, FEATURES], U8, align_bytes=64)
         dz_codes = resident.tile([P, PATHS, CHUNKS, BATCH], U32, align_bytes=64)
         dz_scales = resident.tile([P, PATHS, CHUNKS, BATCH], U8, align_bytes=64)
 
+        saved_tiles = {}
         w_raw = {}
-        chunk_inputs = {}
+        w_grouped = {}
 
         def load_chunk(c):
             grad = saved.tile([P, PACK, BATCH], BF16, name="grad")
             gate = saved.tile([P, PACK, BATCH], F32, name="gate")
             cand = saved.tile([P, PACK, BATCH], F32, name="cand")
-            nc.sync.dma_start(out=grad[:], in_=rows_to_partitions(grad_out, c))
-            nc.sync.dma_start(out=gate[:], in_=rows_to_partitions(gate_i, c))
-            nc.sync.dma_start(out=cand[:], in_=rows_to_partitions(cand_g, c))
-            chunk_inputs[c] = (grad, gate, cand)
+            saved_tiles[c] = (grad, gate, cand)
+            for half in range(HALVES):
+                rows = slice(half * ROWS_IN_HALF, (half + 1) * ROWS_IN_HALF)
+                nc.sync.dma_start(out=grad[:, rows, :], in_=rows_to_partitions(grad_out, c)[:, rows, :])
+                nc.sync.dma_start(out=gate[:, rows, :], in_=rows_to_partitions(gate_i, c)[:, rows, :])
+                nc.sync.dma_start(out=cand[:, rows, :], in_=rows_to_partitions(cand_g, c)[:, rows, :])
+            width = len(FIRST_ROUND_PIECES) * PIECE
             for path in (CANDIDATE, INPUT_GATE):
-                w_raw[path, c] = resident.tile([P, PACK, FEATURES], BF16, name="w_raw_%d_%d" % (path, c))
-                nc.sync.dma_start(out=w_raw[path, c][:], in_=rows_to_partitions(weights[path], c))
+                raw = saved.tile([P, PACK, width], BF16, name="w_first_round", bufs=PATHS * CHUNKS_AHEAD)
+                nc.sync.dma_start(out=raw[:], in_=rows_to_partitions(weights[path], c)[:, :, 0:width])
+                for piece in FIRST_ROUND_PIECES:
+                    w_raw[path, c, piece] = raw[:, :, piece * PIECE : (piece + 1) * PIECE]
 
-        def quantise_weights(path, c, piece, copy, tag, bufs):
+        def load_second_round_weights():
+            cols = slice(SECOND_ROUND_PIECE * PIECE, (SECOND_ROUND_PIECE + 1) * PIECE)
+            for c in range(CHUNKS):
+                for path in (INPUT_GATE, CANDIDATE):
+                    raw = resident.tile([P, PACK, PIECE], BF16, name="w_second_round_%d_%d" % (path, c))
+                    nc.sync.dma_start(out=raw[:], in_=rows_to_partitions(weights[path], c)[:, :, cols])
+                    w_raw[path, c, SECOND_ROUND_PIECE] = raw[:]
+
+        def regroup_on_scalar(path, c, piece):
+            columns = grouped.tile([P, PIECE, PACK], BF16, name="w_by_scalar", bufs=4, align_bytes=64)
+            nc.scalar.copy(out=by_column(columns[:]), in_=by_row(w_raw[path, c, piece]))
+            w_grouped[path, c, piece] = columns
+
+        def regroup_on_vector(path, c, piece):
+            columns = grouped.tile([P, PIECE, PACK], BF16, name="w_by_vector", bufs=2, align_bytes=64)
+            nc.vector.tensor_copy(out=by_column(columns[:]), in_=by_row(w_raw[path, c, piece]))
+            w_grouped[path, c, piece] = columns
+
+        def quantise_weights(path, c, piece):
             cols = slice(piece * PIECE, (piece + 1) * PIECE)
-            w_grouped = grouped.tile([P, PIECE, PACK], BF16, name=tag, bufs=bufs, align_bytes=64)
-            copy(out=by_column(w_grouped[:]), in_=by_row(w_raw[path, c][:, :, cols]))
             nc.vector.quantize_mx(
                 out=w_codes[:, path, c, cols].bitcast(E4M3_X4),
                 scales=w_scales[:, path, c, cols],
-                in_=w_grouped[:].rearrange("p w j -> p (w j)"),
+                in_=w_grouped[path, c, piece][:].rearrange("p w j -> p (w j)"),
             )
 
-        def quantise_dz(path, c, dz_grouped):
+        def quantise_dz(path, c, dz):
             nc.vector.quantize_mx(
                 out=dz_codes[:, path, c, :].bitcast(E5M2_X4),
                 scales=dz_scales[:, path, c, :],
-                in_=dz_grouped[:].rearrange("p w j -> p (w j)"),
+                in_=dz[:].rearrange("p w j -> p (w j)"),
             )
 
-        def multiply(path, c, pieces, sums):
-            for piece in pieces:
-                for t in range(piece * TILES_IN_PIECE, (piece + 1) * TILES_IN_PIECE):
-                    cols = slice(t * P, (t + 1) * P)
-                    nc.tensor.matmul_mx(
-                        out=sums[t][:],
-                        lhsT=w_codes[:, path, c, cols].bitcast(E4M3_X4),
-                        lhsT_scale=w_scales[:, path, c, cols],
-                        rhs=dz_codes[:, path, c, :].bitcast(E5M2_X4),
-                        rhs_scale=dz_scales[:, path, c, :],
-                        start=(c == 0 and path == CANDIDATE),
-                        stop=(c == CHUNKS - 1 and path == INPUT_GATE),
-                    )
+        def multiply(path, c, piece, sums, start, stop):
+            for t in tiles_of(piece):
+                cols = slice(t * P, (t + 1) * P)
+                nc.tensor.matmul_mx(
+                    out=sums[t][:],
+                    lhsT=w_codes[:, path, c, cols].bitcast(E4M3_X4),
+                    lhsT_scale=w_scales[:, path, c, cols],
+                    rhs=dz_codes[:, path, c, :].bitcast(E5M2_X4),
+                    rhs_scale=dz_scales[:, path, c, :],
+                    start=start,
+                    stop=stop,
+                )
 
         def open_sums(pieces):
             sums = {}
             for piece in pieces:
-                for t in range(piece * TILES_IN_PIECE, (piece + 1) * TILES_IN_PIECE):
+                for t in tiles_of(piece):
                     sums[t] = banks.tile([P, BATCH], F32, name="sum")
             return sums
 
-        def store_sums(sums):
-            for t in sorted(sums):
-                result = results.tile([P, BATCH], F32, name="result")
-                if t % 2 == 0:
-                    nc.scalar.copy(out=result[:], in_=sums[t][:])
-                else:
-                    nc.vector.tensor_copy(out=result[:], in_=sums[t][:])
-                nc.sync.dma_start(out=out[t * P : (t + 1) * P, :], in_=result[:])
+        def store(t, sums, copy):
+            result = results.tile([P, BATCH], F32, name="result")
+            copy(out=result[:], in_=sums[t][:])
+            nc.sync.dma_start(out=out[t * P : (t + 1) * P, :], in_=result[:])
 
+        for c in range(CHUNKS_AHEAD):
+            load_chunk(c)
         sums = open_sums(FIRST_ROUND_PIECES)
-        load_chunk(0)
-        for c in range(CHUNKS):
-            if c + 1 < CHUNKS:
-                load_chunk(c + 1)
-            grad, gate, cand = chunk_inputs[c]
 
+        for c in range(CHUNKS):
+            grad, gate, cand = saved_tiles[c]
             cand_sq = scratch.tile([P, PACK, BATCH], F32, name="cand_sq", bufs=2)
-            nc.scalar.activation(out=cand_sq[:], in_=cand[:], func=SQUARE)
             neg_gi = scratch.tile([P, PACK, BATCH], F32, name="neg_gi")
-            nc.vector.scalar_tensor_tensor(
-                out=neg_gi[:], in0=gate[:], scalar=-1.0, in1=grad[:], op0=MULT, op1=MULT
-            )
-            nc.vector.scalar_tensor_tensor(
-                out=gate[:], in0=gate[:], scalar=1.0, in1=cand[:], op0=SUBTRACT, op1=MULT
-            )
+
+            for half in range(HALVES):
+                rows = slice(half * ROWS_IN_HALF, (half + 1) * ROWS_IN_HALF)
+                nc.scalar.activation(out=cand_sq[:, rows, :], in_=cand[:, rows, :], func=SQUARE)
+            for piece in FIRST_ROUND_PIECES:
+                regroup_on_scalar(CANDIDATE, c, piece)
+
+            for half, piece in zip(range(HALVES), FIRST_ROUND_PIECES):
+                rows = slice(half * ROWS_IN_HALF, (half + 1) * ROWS_IN_HALF)
+                nc.vector.scalar_tensor_tensor(
+                    out=neg_gi[:, rows, :], in0=gate[:, rows, :], scalar=-1.0, in1=grad[:, rows, :], op0=MULT, op1=MULT
+                )
+                if c > 0:
+                    quantise_weights(INPUT_GATE, c - 1, piece)
+                    multiply(INPUT_GATE, c - 1, piece, sums, start=False, stop=False)
+                nc.vector.scalar_tensor_tensor(
+                    out=gate[:, rows, :], in0=gate[:, rows, :], scalar=1.0, in1=cand[:, rows, :], op0=SUBTRACT, op1=MULT
+                )
+            for piece in FIRST_ROUND_PIECES:
+                regroup_on_scalar(INPUT_GATE, c, piece)
+
             dzg = grouped.tile([P, BATCH, PACK], BF16, name="dzg", align_bytes=64)
             nc.vector.scalar_tensor_tensor(
                 out=dzg[:],
@@ -153,23 +191,45 @@ def tile_naivelstm_pa_v_kernel(
                 op0=SUBTRACT,
                 op1=MULT,
             )
-            for piece in FIRST_ROUND_PIECES:
-                quantise_weights(CANDIDATE, c, piece, nc.scalar.copy, "w_first", 3)
-            quantise_dz(CANDIDATE, c, dzg)
             dzi = grouped.tile([P, BATCH, PACK], BF16, name="dzi", align_bytes=64)
             nc.vector.tensor_tensor(out=by_column(dzi[:]), in0=by_row(neg_gi[:]), in1=by_row(gate[:]), op=MULT)
-            multiply(CANDIDATE, c, FIRST_ROUND_PIECES, sums)
-            for piece in FIRST_ROUND_PIECES:
-                quantise_weights(INPUT_GATE, c, piece, nc.scalar.copy, "w_first", 3)
+            quantise_dz(CANDIDATE, c, dzg)
+            quantise_weights(CANDIDATE, c, FIRST_ROUND_PIECES[0])
             quantise_dz(INPUT_GATE, c, dzi)
-            multiply(INPUT_GATE, c, FIRST_ROUND_PIECES, sums)
-        store_sums(sums)
+            quantise_weights(CANDIDATE, c, FIRST_ROUND_PIECES[1])
+            for piece in FIRST_ROUND_PIECES:
+                multiply(CANDIDATE, c, piece, sums, start=(c == 0), stop=False)
 
-        sums = open_sums(SECOND_ROUND_PIECES)
-        for c in range(CHUNKS):
-            for piece in SECOND_ROUND_PIECES:
-                quantise_weights(CANDIDATE, c, piece, nc.scalar.copy, "w_second", 2)
-                quantise_weights(INPUT_GATE, c, piece, nc.vector.tensor_copy, "w_second", 2)
-            multiply(CANDIDATE, c, SECOND_ROUND_PIECES, sums)
-            multiply(INPUT_GATE, c, SECOND_ROUND_PIECES, sums)
-        store_sums(sums)
+            if c + CHUNKS_AHEAD < CHUNKS:
+                load_chunk(c + CHUNKS_AHEAD)
+            if c + CHUNKS_AHEAD == CHUNKS - 1:
+                load_second_round_weights()
+
+        vector_units = [(INPUT_GATE, c) for c in range(CHUNKS)] + [(CANDIDATE, CHUNKS - 1)]
+        scalar_units = [(CANDIDATE, c) for c in range(CHUNKS - 1)]
+
+        quantise_weights(INPUT_GATE, CHUNKS - 1, FIRST_ROUND_PIECES[0])
+        regroup_on_vector(vector_units[0][0], vector_units[0][1], SECOND_ROUND_PIECE)
+        quantise_weights(INPUT_GATE, CHUNKS - 1, FIRST_ROUND_PIECES[1])
+        for piece in FIRST_ROUND_PIECES:
+            multiply(INPUT_GATE, CHUNKS - 1, piece, sums, start=False, stop=True)
+
+
+        for t in tiles_of(FIRST_ROUND_PIECES[0]):
+            store(t, sums, nc.scalar.copy)
+        for path, c in scalar_units:
+            regroup_on_scalar(path, c, SECOND_ROUND_PIECE)
+        for t in tiles_of(FIRST_ROUND_PIECES[1]):
+            store(t, sums, nc.scalar.copy)
+
+        sums = open_sums([SECOND_ROUND_PIECE])
+        for n, (path, c) in enumerate(vector_units):
+            if n + 1 < len(vector_units):
+                regroup_on_vector(vector_units[n + 1][0], vector_units[n + 1][1], SECOND_ROUND_PIECE)
+            quantise_weights(path, c, SECOND_ROUND_PIECE)
+            multiply(path, c, SECOND_ROUND_PIECE, sums, start=(n == 0), stop=False)
+        for n, (path, c) in enumerate(scalar_units):
+            quantise_weights(path, c, SECOND_ROUND_PIECE)
+            multiply(path, c, SECOND_ROUND_PIECE, sums, start=False, stop=(n == len(scalar_units) - 1))
+        for t in tiles_of(SECOND_ROUND_PIECE):
+            store(t, sums, nc.scalar.copy if t % 2 == 0 else nc.vector.tensor_copy)

@@ -205,31 +205,36 @@ def tile_naivelstm_pa_v_kernel(
             if c + CHUNKS_AHEAD == CHUNKS - 1:
                 load_second_round_weights()
 
-        vector_units = [(INPUT_GATE, c) for c in range(CHUNKS)] + [(CANDIDATE, CHUNKS - 1)]
-        scalar_units = [(CANDIDATE, c) for c in range(CHUNKS - 1)]
+        ahead = [(INPUT_GATE, 0), (INPUT_GATE, 1)]
+        scalar_unit = (CANDIDATE, 0)
 
-        quantise_weights(INPUT_GATE, CHUNKS - 1, FIRST_ROUND_PIECES[0])
-        regroup_on_vector(vector_units[0][0], vector_units[0][1], SECOND_ROUND_PIECE)
-        quantise_weights(INPUT_GATE, CHUNKS - 1, FIRST_ROUND_PIECES[1])
+        for (path, c), piece in zip(ahead, FIRST_ROUND_PIECES):
+            regroup_on_vector(path, c, SECOND_ROUND_PIECE)
+            quantise_weights(INPUT_GATE, CHUNKS - 1, piece)
         for piece in FIRST_ROUND_PIECES:
             multiply(INPUT_GATE, CHUNKS - 1, piece, sums, start=False, stop=True)
 
 
         for t in tiles_of(FIRST_ROUND_PIECES[0]):
             store(t, sums, nc.scalar.copy)
-        for path, c in scalar_units:
-            regroup_on_scalar(path, c, SECOND_ROUND_PIECE)
+        regroup_on_scalar(scalar_unit[0], scalar_unit[1], SECOND_ROUND_PIECE)
         for t in tiles_of(FIRST_ROUND_PIECES[1]):
             store(t, sums, nc.scalar.copy)
 
         sums = open_sums([SECOND_ROUND_PIECE])
-        for n, (path, c) in enumerate(vector_units):
-            if n + 1 < len(vector_units):
-                regroup_on_vector(vector_units[n + 1][0], vector_units[n + 1][1], SECOND_ROUND_PIECE)
+
+        def finish(path, c, start=False, stop=False):
             quantise_weights(path, c, SECOND_ROUND_PIECE)
-            multiply(path, c, SECOND_ROUND_PIECE, sums, start=(n == 0), stop=False)
-        for n, (path, c) in enumerate(scalar_units):
-            quantise_weights(path, c, SECOND_ROUND_PIECE)
-            multiply(path, c, SECOND_ROUND_PIECE, sums, start=False, stop=(n == len(scalar_units) - 1))
+            multiply(path, c, SECOND_ROUND_PIECE, sums, start=start, stop=stop)
+
+        finish(INPUT_GATE, 0, start=True)
+        finish(INPUT_GATE, 1)
+        regroup_on_vector(INPUT_GATE, 2, SECOND_ROUND_PIECE)
+        finish(INPUT_GATE, 2)
+        regroup_on_vector(CANDIDATE, 2, SECOND_ROUND_PIECE)
+        finish(scalar_unit[0], scalar_unit[1])
+        finish(CANDIDATE, 2)
+        regroup_on_vector(CANDIDATE, 1, SECOND_ROUND_PIECE)
+        finish(CANDIDATE, 1, stop=True)
         for t in tiles_of(SECOND_ROUND_PIECE):
             store(t, sums, nc.scalar.copy if t % 2 == 0 else nc.vector.tensor_copy)

@@ -23,8 +23,7 @@ PIECE = 512
 TILES_IN_PIECE = PIECE // P
 PSUM_BANKS = 8
 RUN = 4
-HALVES = 2
-ROWS_IN_HALF = PACK // HALVES
+ROW_GROUPS = {0: 4, 1: 2, 2: 2}
 CHUNKS_AHEAD = 2
 
 PATHS = 2
@@ -48,6 +47,11 @@ def by_row(tile_view):
 
 def by_column(tile_view):
     return tile_view.rearrange("p (c r) j -> p c j r", r=RUN)
+
+
+def row_groups_of(c):
+    size = PACK // ROW_GROUPS[c]
+    return [slice(g * size, (g + 1) * size) for g in range(ROW_GROUPS[c])]
 
 
 def tiles_of(piece):
@@ -83,8 +87,7 @@ def tile_naivelstm_pa_v_kernel(
             gate = saved.tile([P, PACK, BATCH], F32, name="gate")
             cand = saved.tile([P, PACK, BATCH], F32, name="cand")
             saved_tiles[c] = (grad, gate, cand)
-            for half in range(HALVES):
-                rows = slice(half * ROWS_IN_HALF, (half + 1) * ROWS_IN_HALF)
+            for rows in row_groups_of(c):
                 nc.sync.dma_start(out=grad[:, rows, :], in_=rows_to_partitions(grad_out, c)[:, rows, :])
                 nc.sync.dma_start(out=gate[:, rows, :], in_=rows_to_partitions(gate_i, c)[:, rows, :])
                 nc.sync.dma_start(out=cand[:, rows, :], in_=rows_to_partitions(cand_g, c)[:, rows, :])
@@ -162,20 +165,21 @@ def tile_naivelstm_pa_v_kernel(
             cand_sq = scratch.tile([P, PACK, BATCH], F32, name="cand_sq", bufs=2)
             neg_gi = scratch.tile([P, PACK, BATCH], F32, name="neg_gi")
 
-            for half in range(HALVES):
-                rows = slice(half * ROWS_IN_HALF, (half + 1) * ROWS_IN_HALF)
+            for rows in row_groups_of(c):
                 nc.scalar.activation(out=cand_sq[:, rows, :], in_=cand[:, rows, :], func=SQUARE)
             for piece in FIRST_ROUND_PIECES:
                 regroup_on_scalar(CANDIDATE, c, piece)
 
-            for half, piece in zip(range(HALVES), FIRST_ROUND_PIECES):
-                rows = slice(half * ROWS_IN_HALF, (half + 1) * ROWS_IN_HALF)
-                nc.vector.scalar_tensor_tensor(
-                    out=neg_gi[:, rows, :], in0=gate[:, rows, :], scalar=-1.0, in1=grad[:, rows, :], op0=MULT, op1=MULT
-                )
+            def late_piece(piece):
                 if c > 0:
                     quantise_weights(INPUT_GATE, c - 1, piece)
                     multiply(INPUT_GATE, c - 1, piece, sums, start=False, stop=False)
+
+            for n, rows in enumerate(row_groups_of(c)):
+                nc.vector.scalar_tensor_tensor(
+                    out=neg_gi[:, rows, :], in0=gate[:, rows, :], scalar=-1.0, in1=grad[:, rows, :], op0=MULT, op1=MULT
+                )
+                late_piece(FIRST_ROUND_PIECES[n % len(FIRST_ROUND_PIECES)])
                 nc.vector.scalar_tensor_tensor(
                     out=gate[:, rows, :], in0=gate[:, rows, :], scalar=1.0, in1=cand[:, rows, :], op0=SUBTRACT, op1=MULT
                 )
@@ -206,20 +210,19 @@ def tile_naivelstm_pa_v_kernel(
                 load_second_round_weights()
 
         ahead = [(INPUT_GATE, 0), (INPUT_GATE, 1)]
-        scalar_unit = (CANDIDATE, 0)
+        scalar_units = [(CANDIDATE, 0), (CANDIDATE, 1)]
 
         for (path, c), piece in zip(ahead, FIRST_ROUND_PIECES):
-            regroup_on_vector(path, c, SECOND_ROUND_PIECE)
             quantise_weights(INPUT_GATE, CHUNKS - 1, piece)
+            regroup_on_vector(path, c, SECOND_ROUND_PIECE)
         for piece in FIRST_ROUND_PIECES:
             multiply(INPUT_GATE, CHUNKS - 1, piece, sums, start=False, stop=True)
 
 
-        for t in tiles_of(FIRST_ROUND_PIECES[0]):
-            store(t, sums, nc.scalar.copy)
-        regroup_on_scalar(scalar_unit[0], scalar_unit[1], SECOND_ROUND_PIECE)
-        for t in tiles_of(FIRST_ROUND_PIECES[1]):
-            store(t, sums, nc.scalar.copy)
+        for (path, c), piece in zip(scalar_units, FIRST_ROUND_PIECES):
+            regroup_on_scalar(path, c, SECOND_ROUND_PIECE)
+            for t in tiles_of(piece):
+                store(t, sums, nc.scalar.copy)
 
         sums = open_sums([SECOND_ROUND_PIECE])
 
@@ -230,11 +233,10 @@ def tile_naivelstm_pa_v_kernel(
         finish(INPUT_GATE, 0, start=True)
         finish(INPUT_GATE, 1)
         regroup_on_vector(INPUT_GATE, 2, SECOND_ROUND_PIECE)
+        finish(CANDIDATE, 0)
         finish(INPUT_GATE, 2)
+        finish(CANDIDATE, 1)
         regroup_on_vector(CANDIDATE, 2, SECOND_ROUND_PIECE)
-        finish(scalar_unit[0], scalar_unit[1])
-        finish(CANDIDATE, 2)
-        regroup_on_vector(CANDIDATE, 1, SECOND_ROUND_PIECE)
-        finish(CANDIDATE, 1, stop=True)
+        finish(CANDIDATE, 2, stop=True)
         for t in tiles_of(SECOND_ROUND_PIECE):
             store(t, sums, nc.scalar.copy if t % 2 == 0 else nc.vector.tensor_copy)

@@ -175,34 +175,64 @@ def tile_naivelstm_pa_v_kernel(
                     quantise_weights(INPUT_GATE, c - 1, piece)
                     multiply(INPUT_GATE, c - 1, piece, sums, start=False, stop=False)
 
-            for n, rows in enumerate(row_groups_of(c)):
+            def make_neg_gi(rows):
                 nc.vector.scalar_tensor_tensor(
                     out=neg_gi[:, rows, :], in0=gate[:, rows, :], scalar=-1.0, in1=grad[:, rows, :], op0=MULT, op1=MULT
                 )
-                late_piece(FIRST_ROUND_PIECES[n % len(FIRST_ROUND_PIECES)])
+
+            def make_gate_product(rows):
                 nc.vector.scalar_tensor_tensor(
                     out=gate[:, rows, :], in0=gate[:, rows, :], scalar=1.0, in1=cand[:, rows, :], op0=SUBTRACT, op1=MULT
                 )
-            for piece in FIRST_ROUND_PIECES:
-                regroup_on_scalar(INPUT_GATE, c, piece)
 
             dzg = grouped.tile([P, BATCH, PACK], BF16, name="dzg", align_bytes=64)
-            nc.vector.scalar_tensor_tensor(
-                out=dzg[:],
-                in0=cand_sq[:].rearrange("p j w -> p w j"),
-                scalar=1.0,
-                in1=neg_gi[:].rearrange("p j w -> p w j"),
-                op0=SUBTRACT,
-                op1=MULT,
-            )
             dzi = grouped.tile([P, BATCH, PACK], BF16, name="dzi", align_bytes=64)
-            nc.vector.tensor_tensor(out=by_column(dzi[:]), in0=by_row(neg_gi[:]), in1=by_row(gate[:]), op=MULT)
-            quantise_dz(CANDIDATE, c, dzg)
-            quantise_weights(CANDIDATE, c, FIRST_ROUND_PIECES[0])
-            quantise_dz(INPUT_GATE, c, dzi)
-            quantise_weights(CANDIDATE, c, FIRST_ROUND_PIECES[1])
-            for piece in FIRST_ROUND_PIECES:
+
+            def make_dzg():
+                nc.vector.scalar_tensor_tensor(
+                    out=dzg[:],
+                    in0=cand_sq[:].rearrange("p j w -> p w j"),
+                    scalar=1.0,
+                    in1=neg_gi[:].rearrange("p j w -> p w j"),
+                    op0=SUBTRACT,
+                    op1=MULT,
+                )
+
+            def make_dzi():
+                nc.vector.tensor_tensor(out=by_column(dzi[:]), in0=by_row(neg_gi[:]), in1=by_row(gate[:]), op=MULT)
+
+            def candidate_piece(piece):
+                quantise_weights(CANDIDATE, c, piece)
                 multiply(CANDIDATE, c, piece, sums, start=(c == 0), stop=False)
+
+            groups = row_groups_of(c)
+            if c < CHUNKS - 1:
+                for n, rows in enumerate(groups):
+                    make_neg_gi(rows)
+                    late_piece(FIRST_ROUND_PIECES[n % len(FIRST_ROUND_PIECES)])
+                    make_gate_product(rows)
+                make_dzg()
+                make_dzi()
+                quantise_dz(CANDIDATE, c, dzg)
+                quantise_weights(CANDIDATE, c, FIRST_ROUND_PIECES[0])
+                quantise_dz(INPUT_GATE, c, dzi)
+                quantise_weights(CANDIDATE, c, FIRST_ROUND_PIECES[1])
+                for piece in FIRST_ROUND_PIECES:
+                    multiply(CANDIDATE, c, piece, sums, start=(c == 0), stop=False)
+            else:
+                for rows, piece in zip(groups, FIRST_ROUND_PIECES):
+                    make_neg_gi(rows)
+                    late_piece(piece)
+                make_dzg()
+                make_gate_product(groups[0])
+                quantise_dz(CANDIDATE, c, dzg)
+                make_gate_product(groups[1])
+                candidate_piece(FIRST_ROUND_PIECES[0])
+                make_dzi()
+                candidate_piece(FIRST_ROUND_PIECES[1])
+                quantise_dz(INPUT_GATE, c, dzi)
+            for piece in FIRST_ROUND_PIECES:
+                regroup_on_scalar(INPUT_GATE, c, piece)
 
             if c + CHUNKS_AHEAD < CHUNKS:
                 load_chunk(c + CHUNKS_AHEAD)
@@ -239,4 +269,4 @@ def tile_naivelstm_pa_v_kernel(
         regroup_on_vector(CANDIDATE, 2, SECOND_ROUND_PIECE)
         finish(CANDIDATE, 2, stop=True)
         for t in tiles_of(SECOND_ROUND_PIECE):
-            store(t, sums, nc.scalar.copy if t % 2 == 0 else nc.vector.tensor_copy)
+            store(t, sums, nc.vector.tensor_copy if t % 2 == 0 else nc.scalar.copy)

@@ -1,6 +1,7 @@
 from contextlib import ExitStack
 
 import concourse.mybir as mybir
+from concourse.masks import make_identity
 
 F32 = mybir.dt.float32
 BF16 = mybir.dt.bfloat16
@@ -21,6 +22,7 @@ BATCH = 512
 CHUNKS = HIDDEN // K_PASS
 PIECE = 512
 TILES_IN_PIECE = PIECE // P
+HALF_PIECE = PIECE // 2
 PSUM_BANKS = 8
 RUN = 4
 ROW_GROUPS = {0: 4, 1: 2, 2: 2}
@@ -73,6 +75,9 @@ def tile_naivelstm_pa_v_kernel(
         banks = stack.enter_context(tc.psum_pool(name="banks", bufs=PSUM_BANKS))
         stack.enter_context(tc.manual_schedule())
 
+        identity = resident.tile([P, P], BF16, name="identity")
+        make_identity(nc, identity[:])
+
         w_codes = resident.tile([P, PATHS, CHUNKS, FEATURES], U32, align_bytes=64)
         w_scales = resident.tile([P, PATHS, CHUNKS, FEATURES], U8, align_bytes=64)
         dz_codes = resident.tile([P, PATHS, CHUNKS, BATCH], U32, align_bytes=64)
@@ -82,7 +87,7 @@ def tile_naivelstm_pa_v_kernel(
         w_raw = {}
         w_grouped = {}
 
-        def load_chunk(c):
+        def load_saved(c):
             grad = saved.tile([P, PACK, BATCH], BF16, name="grad")
             gate = saved.tile([P, PACK, BATCH], F32, name="gate")
             cand = saved.tile([P, PACK, BATCH], F32, name="cand")
@@ -91,6 +96,8 @@ def tile_naivelstm_pa_v_kernel(
                 nc.sync.dma_start(out=grad[:, rows, :], in_=rows_to_partitions(grad_out, c)[:, rows, :])
                 nc.sync.dma_start(out=gate[:, rows, :], in_=rows_to_partitions(gate_i, c)[:, rows, :])
                 nc.sync.dma_start(out=cand[:, rows, :], in_=rows_to_partitions(cand_g, c)[:, rows, :])
+
+        def load_first_round(c):
             width = len(FIRST_ROUND_PIECES) * PIECE
             for path in (CANDIDATE, INPUT_GATE):
                 raw = saved.tile([P, PACK, width], BF16, name="w_first_round", bufs=PATHS * CHUNKS_AHEAD)
@@ -98,18 +105,45 @@ def tile_naivelstm_pa_v_kernel(
                 for piece in FIRST_ROUND_PIECES:
                     w_raw[path, c, piece] = raw[:, :, piece * PIECE : (piece + 1) * PIECE]
 
-        def load_second_round_weights():
+        def load_second_round(path, c):
             cols = slice(SECOND_ROUND_PIECE * PIECE, (SECOND_ROUND_PIECE + 1) * PIECE)
-            for c in range(CHUNKS):
-                for path in (INPUT_GATE, CANDIDATE):
-                    raw = resident.tile([P, PACK, PIECE], BF16, name="w_second_round_%d_%d" % (path, c))
-                    nc.sync.dma_start(out=raw[:], in_=rows_to_partitions(weights[path], c)[:, :, cols])
-                    w_raw[path, c, SECOND_ROUND_PIECE] = raw[:]
+            raw = saved.tile([P, PACK, PIECE], BF16, name="w_second_round", bufs=PATHS * CHUNKS_AHEAD)
+            nc.sync.dma_start(out=raw[:], in_=rows_to_partitions(weights[path], c)[:, :, cols])
+            w_raw[path, c, SECOND_ROUND_PIECE] = raw[:]
 
         def regroup_on_scalar(path, c, piece):
             columns = grouped.tile([P, PIECE, PACK], BF16, name="w_by_scalar", bufs=4, align_bytes=64)
             nc.scalar.copy(out=by_column(columns[:]), in_=by_row(w_raw[path, c, piece]))
             w_grouped[path, c, piece] = columns
+
+        def regroup_early_on_scalar(path, c, piece):
+            columns = grouped.tile([P, PIECE, PACK], BF16, name="w_early", bufs=1, align_bytes=64)
+            nc.scalar.copy(out=by_column(columns[:]), in_=by_row(w_raw[path, c, piece]))
+            w_grouped[path, c, piece] = columns
+
+        def regroup_on_tensor(path, c, piece):
+            columns = grouped.tile([P, PIECE, PACK], BF16, name="w_by_scalar", bufs=4, align_bytes=64)
+            raw = w_raw[path, c, piece]
+            for h in range(2):
+                cols = slice(h * HALF_PIECE, (h + 1) * HALF_PIECE)
+                bank = banks.tile([P, HALF_PIECE, PACK], BF16, name="sum")
+                for j in range(0, PACK, 2):
+                    nc.tensor.matmul(
+                        out=bank[:, :, j : j + 2].rearrange("p w j -> p j w"),
+                        lhsT=identity[:],
+                        rhs=raw[:, j : j + 2, cols],
+                        start=True,
+                        stop=True,
+                    )
+                nc.scalar.copy(out=columns[:, cols, :], in_=bank[:])
+            w_grouped[path, c, piece] = columns
+
+        def regroup_pair(path, c):
+            regroup_on_scalar(path, c, FIRST_ROUND_PIECES[0])
+            if c < 2:
+                regroup_on_tensor(path, c, FIRST_ROUND_PIECES[1])
+            else:
+                regroup_on_scalar(path, c, FIRST_ROUND_PIECES[1])
 
         def regroup_on_vector(path, c, piece):
             columns = grouped.tile([P, PIECE, PACK], BF16, name="w_by_vector", bufs=2, align_bytes=64)
@@ -157,8 +191,8 @@ def tile_naivelstm_pa_v_kernel(
             nc.sync.dma_start(out=out[t * P : (t + 1) * P, :], in_=result[:])
 
         for c in range(CHUNKS_AHEAD):
-            load_chunk(c)
-        sums = open_sums(FIRST_ROUND_PIECES)
+            load_saved(c)
+            load_first_round(c)
 
         for c in range(CHUNKS):
             grad, gate, cand = saved_tiles[c]
@@ -167,12 +201,16 @@ def tile_naivelstm_pa_v_kernel(
 
             for rows in row_groups_of(c):
                 nc.scalar.activation(out=cand_sq[:, rows, :], in_=cand[:, rows, :], func=SQUARE)
-            for piece in FIRST_ROUND_PIECES:
-                regroup_on_scalar(CANDIDATE, c, piece)
+            if c == 2:
+                regroup_early_on_scalar(INPUT_GATE, 0, SECOND_ROUND_PIECE)
+            regroup_pair(CANDIDATE, c)
+            if c == 0:
+                regroup_pair(INPUT_GATE, c)
 
             def late_piece(piece):
                 if c > 0:
                     quantise_weights(INPUT_GATE, c - 1, piece)
+                if c == 2:
                     multiply(INPUT_GATE, c - 1, piece, sums, start=False, stop=False)
 
             def make_neg_gi(rows):
@@ -217,8 +255,6 @@ def tile_naivelstm_pa_v_kernel(
                 quantise_weights(CANDIDATE, c, FIRST_ROUND_PIECES[0])
                 quantise_dz(INPUT_GATE, c, dzi)
                 quantise_weights(CANDIDATE, c, FIRST_ROUND_PIECES[1])
-                for piece in FIRST_ROUND_PIECES:
-                    multiply(CANDIDATE, c, piece, sums, start=(c == 0), stop=False)
             else:
                 for rows, piece in zip(groups, FIRST_ROUND_PIECES):
                     make_neg_gi(rows)
@@ -231,25 +267,31 @@ def tile_naivelstm_pa_v_kernel(
                 make_dzi()
                 candidate_piece(FIRST_ROUND_PIECES[1])
                 quantise_dz(INPUT_GATE, c, dzi)
-            for piece in FIRST_ROUND_PIECES:
-                regroup_on_scalar(INPUT_GATE, c, piece)
+            if c > 0:
+                regroup_pair(INPUT_GATE, c)
+            if c == 0:
+                load_saved(2)
+                load_second_round(INPUT_GATE, 0)
+                load_first_round(2)
+                load_second_round(CANDIDATE, 0)
+                load_second_round(INPUT_GATE, 1)
+                load_second_round(CANDIDATE, 1)
+            if c == 1:
+                sums = open_sums(FIRST_ROUND_PIECES)
+                for path, cc in ((CANDIDATE, 0), (INPUT_GATE, 0), (CANDIDATE, 1)):
+                    for piece in FIRST_ROUND_PIECES:
+                        multiply(path, cc, piece, sums, start=(path, cc) == (CANDIDATE, 0), stop=False)
+            if c == 2:
+                load_second_round(INPUT_GATE, 2)
+                load_second_round(CANDIDATE, 2)
 
-            if c + CHUNKS_AHEAD < CHUNKS:
-                load_chunk(c + CHUNKS_AHEAD)
-            if c + CHUNKS_AHEAD == CHUNKS - 1:
-                load_second_round_weights()
-
-        ahead = [(INPUT_GATE, 0), (INPUT_GATE, 1)]
-        scalar_units = [(CANDIDATE, 0), (CANDIDATE, 1)]
-
-        for (path, c), piece in zip(ahead, FIRST_ROUND_PIECES):
+        for piece in FIRST_ROUND_PIECES:
             quantise_weights(INPUT_GATE, CHUNKS - 1, piece)
-            regroup_on_vector(path, c, SECOND_ROUND_PIECE)
         for piece in FIRST_ROUND_PIECES:
             multiply(INPUT_GATE, CHUNKS - 1, piece, sums, start=False, stop=True)
 
 
-        for (path, c), piece in zip(scalar_units, FIRST_ROUND_PIECES):
+        for (path, c), piece in zip([(CANDIDATE, 0), (CANDIDATE, 1)], FIRST_ROUND_PIECES):
             regroup_on_scalar(path, c, SECOND_ROUND_PIECE)
             for t in tiles_of(piece):
                 store(t, sums, nc.scalar.copy)
@@ -261,9 +303,10 @@ def tile_naivelstm_pa_v_kernel(
             multiply(path, c, SECOND_ROUND_PIECE, sums, start=start, stop=stop)
 
         finish(INPUT_GATE, 0, start=True)
+        regroup_on_vector(INPUT_GATE, 1, SECOND_ROUND_PIECE)
+        finish(CANDIDATE, 0)
         finish(INPUT_GATE, 1)
         regroup_on_vector(INPUT_GATE, 2, SECOND_ROUND_PIECE)
-        finish(CANDIDATE, 0)
         finish(INPUT_GATE, 2)
         finish(CANDIDATE, 1)
         regroup_on_vector(CANDIDATE, 2, SECOND_ROUND_PIECE)

@@ -12,6 +12,7 @@ E5M2_X4 = mybir.dt.float8_e5m2_x4
 MULT = mybir.AluOpType.mult
 SUBTRACT = mybir.AluOpType.subtract
 SQUARE = mybir.ActivationFunctionType.Square
+COPY = mybir.ActivationFunctionType.Copy
 
 P = 128
 PACK = 4
@@ -25,7 +26,7 @@ TILES_IN_PIECE = PIECE // P
 HALF_PIECE = PIECE // 2
 PSUM_BANKS = 8
 RUN = 4
-ROW_GROUPS = {0: 4, 1: 2, 2: 2}
+ROW_GROUPS = {0: 4, 1: 2, 2: 1}
 CHUNKS_AHEAD = 2
 
 PATHS = 2
@@ -201,6 +202,8 @@ def tile_naivelstm_pa_v_kernel(
 
             for rows in row_groups_of(c):
                 nc.scalar.activation(out=cand_sq[:, rows, :], in_=cand[:, rows, :], func=SQUARE)
+                if c == 0:
+                    nc.scalar.activation(out=cand_sq[:, rows, :], in_=cand_sq[:, rows, :], func=COPY, bias=-1.0)
             if c == 2:
                 regroup_early_on_scalar(INPUT_GATE, 0, SECOND_ROUND_PIECE)
             regroup_pair(CANDIDATE, c)
@@ -236,6 +239,9 @@ def tile_naivelstm_pa_v_kernel(
                     op1=MULT,
                 )
 
+            def make_dzg_from_difference():
+                nc.vector.tensor_tensor(out=by_column(dzg[:]), in0=by_row(cand_sq[:]), in1=by_row(neg_gi[:]), op=MULT)
+
             def make_dzi():
                 nc.vector.tensor_tensor(out=by_column(dzi[:]), in0=by_row(neg_gi[:]), in1=by_row(gate[:]), op=MULT)
 
@@ -249,20 +255,24 @@ def tile_naivelstm_pa_v_kernel(
                     make_neg_gi(rows)
                     late_piece(FIRST_ROUND_PIECES[n % len(FIRST_ROUND_PIECES)])
                     make_gate_product(rows)
-                make_dzg()
-                make_dzi()
-                quantise_dz(CANDIDATE, c, dzg)
-                quantise_weights(CANDIDATE, c, FIRST_ROUND_PIECES[0])
-                quantise_dz(INPUT_GATE, c, dzi)
-                quantise_weights(CANDIDATE, c, FIRST_ROUND_PIECES[1])
+                if c == 0:
+                    make_dzi()
+                    make_dzg_from_difference()
+                    quantised = ((INPUT_GATE, dzi), (CANDIDATE, dzg))
+                else:
+                    make_dzg()
+                    make_dzi()
+                    quantised = ((CANDIDATE, dzg), (INPUT_GATE, dzi))
+                for (path, dz), piece in zip(quantised, FIRST_ROUND_PIECES):
+                    quantise_dz(path, c, dz)
+                    quantise_weights(CANDIDATE, c, piece)
             else:
-                for rows, piece in zip(groups, FIRST_ROUND_PIECES):
-                    make_neg_gi(rows)
+                make_neg_gi(groups[0])
+                for piece in FIRST_ROUND_PIECES:
                     late_piece(piece)
                 make_dzg()
                 make_gate_product(groups[0])
                 quantise_dz(CANDIDATE, c, dzg)
-                make_gate_product(groups[1])
                 candidate_piece(FIRST_ROUND_PIECES[0])
                 make_dzi()
                 candidate_piece(FIRST_ROUND_PIECES[1])

@@ -151,12 +151,12 @@ def tile_naivelstm_pa_v_kernel(
             nc.vector.tensor_copy(out=by_column(columns[:]), in_=by_row(w_raw[path, c, piece]))
             w_grouped[path, c, piece] = columns
 
-        def quantise_weights(path, c, piece):
-            cols = slice(piece * PIECE, (piece + 1) * PIECE)
+        def quantise_weights(path, c, piece, part=slice(0, PIECE)):
+            cols = slice(piece * PIECE + part.start, piece * PIECE + part.stop)
             nc.vector.quantize_mx(
                 out=w_codes[:, path, c, cols].bitcast(E4M3_X4),
                 scales=w_scales[:, path, c, cols],
-                in_=w_grouped[path, c, piece][:].rearrange("p w j -> p (w j)"),
+                in_=w_grouped[path, c, piece][:, part, :].rearrange("p w j -> p (w j)"),
             )
 
         def quantise_dz(path, c, dz):
@@ -166,8 +166,8 @@ def tile_naivelstm_pa_v_kernel(
                 in_=dz[:].rearrange("p w j -> p (w j)"),
             )
 
-        def multiply(path, c, piece, sums, start, stop):
-            for t in tiles_of(piece):
+        def multiply(path, c, tiles, sums, start, stop):
+            for t in tiles:
                 cols = slice(t * P, (t + 1) * P)
                 nc.tensor.matmul_mx(
                     out=sums[t][:],
@@ -214,7 +214,7 @@ def tile_naivelstm_pa_v_kernel(
                 if c > 0:
                     quantise_weights(INPUT_GATE, c - 1, piece)
                 if c == 2:
-                    multiply(INPUT_GATE, c - 1, piece, sums, start=False, stop=False)
+                    multiply(INPUT_GATE, c - 1, tiles_of(piece), sums, start=False, stop=False)
 
             def make_neg_gi(rows):
                 nc.vector.scalar_tensor_tensor(
@@ -247,7 +247,7 @@ def tile_naivelstm_pa_v_kernel(
 
             def candidate_piece(piece):
                 quantise_weights(CANDIDATE, c, piece)
-                multiply(CANDIDATE, c, piece, sums, start=(c == 0), stop=False)
+                multiply(CANDIDATE, c, tiles_of(piece), sums, start=(c == 0), stop=False)
 
             groups = row_groups_of(c)
             if c < CHUNKS - 1:
@@ -290,7 +290,7 @@ def tile_naivelstm_pa_v_kernel(
                 sums = open_sums(FIRST_ROUND_PIECES)
                 for path, cc in ((CANDIDATE, 0), (INPUT_GATE, 0), (CANDIDATE, 1)):
                     for piece in FIRST_ROUND_PIECES:
-                        multiply(path, cc, piece, sums, start=(path, cc) == (CANDIDATE, 0), stop=False)
+                        multiply(path, cc, tiles_of(piece), sums, start=(path, cc) == (CANDIDATE, 0), stop=False)
             if c == 2:
                 load_second_round(INPUT_GATE, 2)
                 load_second_round(CANDIDATE, 2)
@@ -298,7 +298,7 @@ def tile_naivelstm_pa_v_kernel(
         for piece in FIRST_ROUND_PIECES:
             quantise_weights(INPUT_GATE, CHUNKS - 1, piece)
         for piece in FIRST_ROUND_PIECES:
-            multiply(INPUT_GATE, CHUNKS - 1, piece, sums, start=False, stop=True)
+            multiply(INPUT_GATE, CHUNKS - 1, tiles_of(piece), sums, start=False, stop=True)
 
 
         for (path, c), piece in zip([(CANDIDATE, 0), (CANDIDATE, 1)], FIRST_ROUND_PIECES):
@@ -310,7 +310,7 @@ def tile_naivelstm_pa_v_kernel(
 
         def finish(path, c, start=False, stop=False):
             quantise_weights(path, c, SECOND_ROUND_PIECE)
-            multiply(path, c, SECOND_ROUND_PIECE, sums, start=start, stop=stop)
+            multiply(path, c, tiles_of(SECOND_ROUND_PIECE), sums, start=start, stop=stop)
 
         finish(INPUT_GATE, 0, start=True)
         regroup_on_vector(INPUT_GATE, 1, SECOND_ROUND_PIECE)
@@ -318,8 +318,12 @@ def tile_naivelstm_pa_v_kernel(
         finish(INPUT_GATE, 1)
         regroup_on_vector(INPUT_GATE, 2, SECOND_ROUND_PIECE)
         finish(INPUT_GATE, 2)
-        finish(CANDIDATE, 1)
+        quantise_weights(CANDIDATE, 1, SECOND_ROUND_PIECE)
         regroup_on_vector(CANDIDATE, 2, SECOND_ROUND_PIECE)
-        finish(CANDIDATE, 2, stop=True)
+        for h in range(2):
+            tiles = tiles_of(SECOND_ROUND_PIECE)[2 * h : 2 * h + 2]
+            multiply(CANDIDATE, 1, tiles, sums, start=False, stop=False)
+            quantise_weights(CANDIDATE, 2, SECOND_ROUND_PIECE, slice(h * HALF_PIECE, (h + 1) * HALF_PIECE))
+            multiply(CANDIDATE, 2, tiles, sums, start=False, stop=True)
         for t in tiles_of(SECOND_ROUND_PIECE):
             store(t, sums, nc.vector.tensor_copy if t % 2 == 0 else nc.scalar.copy)

@@ -186,10 +186,13 @@ def tile_naivelstm_pa_v_kernel(
                     sums[t] = banks.tile([P, BATCH], F32, name="sum")
             return sums
 
-        def store(t, sums, copy):
+        def store(t, sums, copy, parts=1):
             result = results.tile([P, BATCH], F32, name="result")
-            copy(out=result[:], in_=sums[t][:])
-            nc.sync.dma_start(out=out[t * P : (t + 1) * P, :], in_=result[:])
+            width = BATCH // parts
+            for n in range(parts):
+                cols = slice(n * width, (n + 1) * width)
+                copy(out=result[:, cols], in_=sums[t][:, cols])
+                nc.sync.dma_start(out=out[t * P : (t + 1) * P, cols], in_=result[:, cols])
 
         for c in range(CHUNKS_AHEAD):
             load_saved(c)
@@ -326,4 +329,4 @@ def tile_naivelstm_pa_v_kernel(
             quantise_weights(CANDIDATE, 2, SECOND_ROUND_PIECE, slice(h * HALF_PIECE, (h + 1) * HALF_PIECE))
             multiply(CANDIDATE, 2, tiles, sums, start=False, stop=True)
         for t in tiles_of(SECOND_ROUND_PIECE):
-            store(t, sums, nc.vector.tensor_copy if t % 2 == 0 else nc.scalar.copy)
+            store(t, sums, nc.vector.tensor_copy if t % 2 == 0 else nc.scalar.copy, parts=1 if t < 10 else 2)

@@ -108,7 +108,7 @@ def tile_naivelstm_pa_v_kernel(
 
         def load_second_round(path, c):
             cols = slice(SECOND_ROUND_PIECE * PIECE, (SECOND_ROUND_PIECE + 1) * PIECE)
-            raw = saved.tile([P, PACK, PIECE], BF16, name="w_second_round", bufs=PATHS * CHUNKS_AHEAD)
+            raw = saved.tile([P, PACK, PIECE], BF16, name="w_second_round", bufs=PATHS * CHUNKS)
             nc.sync.dma_start(out=raw[:], in_=rows_to_partitions(weights[path], c)[:, :, cols])
             w_raw[path, c, SECOND_ROUND_PIECE] = raw[:]
 
@@ -318,11 +318,11 @@ def tile_naivelstm_pa_v_kernel(
         finish(INPUT_GATE, 0, start=True)
         regroup_on_vector(INPUT_GATE, 1, SECOND_ROUND_PIECE)
         finish(CANDIDATE, 0)
-        finish(INPUT_GATE, 1)
         regroup_on_vector(INPUT_GATE, 2, SECOND_ROUND_PIECE)
+        finish(INPUT_GATE, 1)
         finish(INPUT_GATE, 2)
-        quantise_weights(CANDIDATE, 1, SECOND_ROUND_PIECE)
         regroup_on_vector(CANDIDATE, 2, SECOND_ROUND_PIECE)
+        quantise_weights(CANDIDATE, 1, SECOND_ROUND_PIECE)
         for h in range(2):
             tiles = tiles_of(SECOND_ROUND_PIECE)[2 * h : 2 * h + 2]
             multiply(CANDIDATE, 1, tiles, sums, start=False, stop=False)

from contextlib import ExitStack

import concourse.mybir as mybir
from concourse.masks import make_identity

F32 = mybir.dt.float32
BF16 = mybir.dt.bfloat16
U32 = mybir.dt.uint32
U8 = mybir.dt.uint8
E4M3_X4 = mybir.dt.float8_e4m3fn_x4
E5M2_X4 = mybir.dt.float8_e5m2_x4
MULT = mybir.AluOpType.mult
SUBTRACT = mybir.AluOpType.subtract
SQUARE = mybir.ActivationFunctionType.Square
COPY = mybir.ActivationFunctionType.Copy

P = 128
PACK = 4
K_PASS = P * PACK
HIDDEN = 1536
FEATURES = 1536
BATCH = 512
CHUNKS = HIDDEN // K_PASS
PIECE = 512
TILES_IN_PIECE = PIECE // P
HALF_PIECE = PIECE // 2
PSUM_BANKS = 8
RUN = 4
ROW_GROUPS = {0: 4, 1: 2, 2: 1}
CHUNKS_AHEAD = 2

PATHS = 2
CANDIDATE = 0
INPUT_GATE = 1

FIRST_ROUND_PIECES = (0, 1)
SECOND_ROUND_PIECE = 2

FLOPS = 2 * PATHS * HIDDEN * FEATURES * BATCH
BYTES = PATHS * HIDDEN * FEATURES * 2 + 2 * HIDDEN * BATCH * 4 + HIDDEN * BATCH * 2 + FEATURES * BATCH * 4


def rows_to_partitions(dram, c):
    return dram[c * K_PASS : (c + 1) * K_PASS, :].rearrange("(p j) w -> p j w", j=PACK)


def by_row(tile_view):
    return tile_view.rearrange("p j (c r) -> p c j r", r=RUN)


def by_column(tile_view):
    return tile_view.rearrange("p (c r) j -> p c j r", r=RUN)


def row_groups_of(c):
    size = PACK // ROW_GROUPS[c]
    return [slice(g * size, (g + 1) * size) for g in range(ROW_GROUPS[c])]


def tiles_of(piece):
    return range(piece * TILES_IN_PIECE, (piece + 1) * TILES_IN_PIECE)


def tile_naivelstm_pa_v_kernel(
    tc, x, h, w_ii, w_ig, w_hi, w_hg, b_ii, b_hi, b_ig, b_hg, gate_i, cand_g, grad_out, out
):
    nc = tc.nc
    weights = {CANDIDATE: w_ig, INPUT_GATE: w_ii}

    with ExitStack() as stack:
        resident = stack.enter_context(tc.tile_pool(name="resident", bufs=1))
        saved = stack.enter_context(tc.tile_pool(name="saved", bufs=CHUNKS_AHEAD))
        scratch = stack.enter_context(tc.tile_pool(name="scratch", bufs=1))
        grouped = stack.enter_context(tc.tile_pool(name="grouped", bufs=1))
        results = stack.enter_context(tc.tile_pool(name="results", bufs=PSUM_BANKS))
        banks = stack.enter_context(tc.psum_pool(name="banks", bufs=PSUM_BANKS))
        stack.enter_context(tc.manual_schedule())

        identity = resident.tile([P, P], BF16, name="identity")
        make_identity(nc, identity[:])

        w_codes = resident.tile([P, PATHS, CHUNKS, FEATURES], U32, align_bytes=64)
        w_scales = resident.tile([P, PATHS, CHUNKS, FEATURES], U8, align_bytes=64)
        dz_codes = resident.tile([P, PATHS, CHUNKS, BATCH], U32, align_bytes=64)
        dz_scales = resident.tile([P, PATHS, CHUNKS, BATCH], U8, align_bytes=64)

        saved_tiles = {}
        w_raw = {}
        w_grouped = {}

        def load_saved(c):
            grad = saved.tile([P, PACK, BATCH], BF16, name="grad")
            gate = saved.tile([P, PACK, BATCH], F32, name="gate")
            cand = saved.tile([P, PACK, BATCH], F32, name="cand")
            saved_tiles[c] = (grad, gate, cand)
            for rows in row_groups_of(c):
                nc.sync.dma_start(out=grad[:, rows, :], in_=rows_to_partitions(grad_out, c)[:, rows, :])
                nc.sync.dma_start(out=gate[:, rows, :], in_=rows_to_partitions(gate_i, c)[:, rows, :])
                nc.sync.dma_start(out=cand[:, rows, :], in_=rows_to_partitions(cand_g, c)[:, rows, :])

        def load_first_round(c):
            width = len(FIRST_ROUND_PIECES) * PIECE
            for path in (CANDIDATE, INPUT_GATE):
                raw = saved.tile([P, PACK, width], BF16, name="w_first_round", bufs=PATHS * CHUNKS_AHEAD)
                nc.sync.dma_start(out=raw[:], in_=rows_to_partitions(weights[path], c)[:, :, 0:width])
                for piece in FIRST_ROUND_PIECES:
                    w_raw[path, c, piece] = raw[:, :, piece * PIECE : (piece + 1) * PIECE]

        def load_second_round(path, c):
            cols = slice(SECOND_ROUND_PIECE * PIECE, (SECOND_ROUND_PIECE + 1) * PIECE)
            raw = saved.tile([P, PACK, PIECE], BF16, name="w_second_round", bufs=PATHS * CHUNKS)
            nc.sync.dma_start(out=raw[:], in_=rows_to_partitions(weights[path], c)[:, :, cols])
            w_raw[path, c, SECOND_ROUND_PIECE] = raw[:]

        def regroup_on_scalar(path, c, piece):
            columns = grouped.tile([P, PIECE, PACK], BF16, name="w_by_scalar", bufs=4, align_bytes=64)
            nc.scalar.copy(out=by_column(columns[:]), in_=by_row(w_raw[path, c, piece]))
            w_grouped[path, c, piece] = columns

        def regroup_early_on_scalar(path, c, piece):
            columns = grouped.tile([P, PIECE, PACK], BF16, name="w_early", bufs=1, align_bytes=64)
            nc.scalar.copy(out=by_column(columns[:]), in_=by_row(w_raw[path, c, piece]))
            w_grouped[path, c, piece] = columns

        def regroup_on_tensor(path, c, piece):
            columns = grouped.tile([P, PIECE, PACK], BF16, name="w_by_scalar", bufs=4, align_bytes=64)
            raw = w_raw[path, c, piece]
            for h in range(2):
                cols = slice(h * HALF_PIECE, (h + 1) * HALF_PIECE)
                bank = banks.tile([P, HALF_PIECE, PACK], BF16, name="sum")
                for j in range(0, PACK, 2):
                    nc.tensor.matmul(
                        out=bank[:, :, j : j + 2].rearrange("p w j -> p j w"),
                        lhsT=identity[:],
                        rhs=raw[:, j : j + 2, cols],
                        start=True,
                        stop=True,
                    )
                nc.scalar.copy(out=columns[:, cols, :], in_=bank[:])
            w_grouped[path, c, piece] = columns

        def regroup_pair(path, c):
            regroup_on_scalar(path, c, FIRST_ROUND_PIECES[0])
            if c < 2:
                regroup_on_tensor(path, c, FIRST_ROUND_PIECES[1])
            else:
                regroup_on_scalar(path, c, FIRST_ROUND_PIECES[1])

        def regroup_on_vector(path, c, piece):
            columns = grouped.tile([P, PIECE, PACK], BF16, name="w_by_vector", bufs=2, align_bytes=64)
            nc.vector.tensor_copy(out=by_column(columns[:]), in_=by_row(w_raw[path, c, piece]))
            w_grouped[path, c, piece] = columns

        def quantise_weights(path, c, piece, part=slice(0, PIECE)):
            cols = slice(piece * PIECE + part.start, piece * PIECE + part.stop)
            nc.vector.quantize_mx(
                out=w_codes[:, path, c, cols].bitcast(E4M3_X4),
                scales=w_scales[:, path, c, cols],
                in_=w_grouped[path, c, piece][:, part, :].rearrange("p w j -> p (w j)"),
            )

        def quantise_dz(path, c, dz):
            nc.vector.quantize_mx(
                out=dz_codes[:, path, c, :].bitcast(E5M2_X4),
                scales=dz_scales[:, path, c, :],
                in_=dz[:].rearrange("p w j -> p (w j)"),
            )

        def multiply(path, c, tiles, sums, start, stop):
            for t in tiles:
                cols = slice(t * P, (t + 1) * P)
                nc.tensor.matmul_mx(
                    out=sums[t][:],
                    lhsT=w_codes[:, path, c, cols].bitcast(E4M3_X4),
                    lhsT_scale=w_scales[:, path, c, cols],
                    rhs=dz_codes[:, path, c, :].bitcast(E5M2_X4),
                    rhs_scale=dz_scales[:, path, c, :],
                    start=start,
                    stop=stop,
                )

        def open_sums(pieces):
            sums = {}
            for piece in pieces:
                for t in tiles_of(piece):
                    sums[t] = banks.tile([P, BATCH], F32, name="sum")
            return sums

        def store(t, sums, copy, parts=1):
            result = results.tile([P, BATCH], F32, name="result")
            width = BATCH // parts
            for n in range(parts):
                cols = slice(n * width, (n + 1) * width)
                copy(out=result[:, cols], in_=sums[t][:, cols])
                nc.sync.dma_start(out=out[t * P : (t + 1) * P, cols], in_=result[:, cols])

        for c in range(CHUNKS_AHEAD):
            load_saved(c)
            load_first_round(c)

        for c in range(CHUNKS):
            grad, gate, cand = saved_tiles[c]
            cand_sq = scratch.tile([P, PACK, BATCH], F32, name="cand_sq", bufs=2)
            neg_gi = scratch.tile([P, PACK, BATCH], F32, name="neg_gi")

            for rows in row_groups_of(c):
                nc.scalar.activation(out=cand_sq[:, rows, :], in_=cand[:, rows, :], func=SQUARE)
                if c == 0:
                    nc.scalar.activation(out=cand_sq[:, rows, :], in_=cand_sq[:, rows, :], func=COPY, bias=-1.0)
            if c == 2:
                regroup_early_on_scalar(INPUT_GATE, 0, SECOND_ROUND_PIECE)
            regroup_pair(CANDIDATE, c)
            if c == 0:
                regroup_pair(INPUT_GATE, c)

            def late_piece(piece):
                if c > 0:
                    quantise_weights(INPUT_GATE, c - 1, piece)
                if c == 2:
                    multiply(INPUT_GATE, c - 1, tiles_of(piece), sums, start=False, stop=False)

            def make_neg_gi(rows):
                nc.vector.scalar_tensor_tensor(
                    out=neg_gi[:, rows, :], in0=gate[:, rows, :], scalar=-1.0, in1=grad[:, rows, :], op0=MULT, op1=MULT
                )

            def make_gate_product(rows):
                nc.vector.scalar_tensor_tensor(
                    out=gate[:, rows, :], in0=gate[:, rows, :], scalar=1.0, in1=cand[:, rows, :], op0=SUBTRACT, op1=MULT
                )

            dzg = grouped.tile([P, BATCH, PACK], BF16, name="dzg", align_bytes=64)
            dzi = grouped.tile([P, BATCH, PACK], BF16, name="dzi", align_bytes=64)

            def make_dzg():
                nc.vector.scalar_tensor_tensor(
                    out=dzg[:],
                    in0=cand_sq[:].rearrange("p j w -> p w j"),
                    scalar=1.0,
                    in1=neg_gi[:].rearrange("p j w -> p w j"),
                    op0=SUBTRACT,
                    op1=MULT,
                )

            def make_dzg_from_difference():
                nc.vector.tensor_tensor(out=by_column(dzg[:]), in0=by_row(cand_sq[:]), in1=by_row(neg_gi[:]), op=MULT)

            def make_dzi():
                nc.vector.tensor_tensor(out=by_column(dzi[:]), in0=by_row(neg_gi[:]), in1=by_row(gate[:]), op=MULT)

            def candidate_piece(piece):
                quantise_weights(CANDIDATE, c, piece)
                multiply(CANDIDATE, c, tiles_of(piece), sums, start=(c == 0), stop=False)

            groups = row_groups_of(c)
            if c < CHUNKS - 1:
                for n, rows in enumerate(groups):
                    make_neg_gi(rows)
                    late_piece(FIRST_ROUND_PIECES[n % len(FIRST_ROUND_PIECES)])
                    make_gate_product(rows)
                if c == 0:
                    make_dzi()
                    make_dzg_from_difference()
                    quantised = ((INPUT_GATE, dzi), (CANDIDATE, dzg))
                else:
                    make_dzg()
                    make_dzi()
                    quantised = ((CANDIDATE, dzg), (INPUT_GATE, dzi))
                for (path, dz), piece in zip(quantised, FIRST_ROUND_PIECES):
                    quantise_dz(path, c, dz)
                    quantise_weights(CANDIDATE, c, piece)
            else:
                make_neg_gi(groups[0])
                for piece in FIRST_ROUND_PIECES:
                    late_piece(piece)
                make_dzg()
                make_gate_product(groups[0])
                quantise_dz(CANDIDATE, c, dzg)
                candidate_piece(FIRST_ROUND_PIECES[0])
                make_dzi()
                candidate_piece(FIRST_ROUND_PIECES[1])
                quantise_dz(INPUT_GATE, c, dzi)
            if c > 0:
                regroup_pair(INPUT_GATE, c)
            if c == 0:
                load_saved(2)
                load_second_round(INPUT_GATE, 0)
                load_first_round(2)
                load_second_round(CANDIDATE, 0)
                load_second_round(INPUT_GATE, 1)
                load_second_round(CANDIDATE, 1)
            if c == 1:
                sums = open_sums(FIRST_ROUND_PIECES)
                for path, cc in ((CANDIDATE, 0), (INPUT_GATE, 0), (CANDIDATE, 1)):
                    for piece in FIRST_ROUND_PIECES:
                        multiply(path, cc, tiles_of(piece), sums, start=(path, cc) == (CANDIDATE, 0), stop=False)
            if c == 2:
                load_second_round(INPUT_GATE, 2)
                load_second_round(CANDIDATE, 2)

        for piece in FIRST_ROUND_PIECES:
            quantise_weights(INPUT_GATE, CHUNKS - 1, piece)
        for piece in FIRST_ROUND_PIECES:
            multiply(INPUT_GATE, CHUNKS - 1, tiles_of(piece), sums, start=False, stop=True)


        for (path, c), piece in zip([(CANDIDATE, 0), (CANDIDATE, 1)], FIRST_ROUND_PIECES):
            regroup_on_scalar(path, c, SECOND_ROUND_PIECE)
            for t in tiles_of(piece):
                store(t, sums, nc.scalar.copy)

        sums = open_sums([SECOND_ROUND_PIECE])

        def finish(path, c, start=False, stop=False):
            quantise_weights(path, c, SECOND_ROUND_PIECE)
            multiply(path, c, tiles_of(SECOND_ROUND_PIECE), sums, start=start, stop=stop)

        finish(INPUT_GATE, 0, start=True)
        regroup_on_vector(INPUT_GATE, 1, SECOND_ROUND_PIECE)
        finish(CANDIDATE, 0)
        regroup_on_vector(INPUT_GATE, 2, SECOND_ROUND_PIECE)
        finish(INPUT_GATE, 1)
        finish(INPUT_GATE, 2)
        regroup_on_vector(CANDIDATE, 2, SECOND_ROUND_PIECE)
        quantise_weights(CANDIDATE, 1, SECOND_ROUND_PIECE)
        for h in range(2):
            tiles = tiles_of(SECOND_ROUND_PIECE)[2 * h : 2 * h + 2]
            multiply(CANDIDATE, 1, tiles, sums, start=False, stop=False)
            quantise_weights(CANDIDATE, 2, SECOND_ROUND_PIECE, slice(h * HALF_PIECE, (h + 1) * HALF_PIECE))
            multiply(CANDIDATE, 2, tiles, sums, start=False, stop=True)
        for t in tiles_of(SECOND_ROUND_PIECE):
            store(t, sums, nc.vector.tensor_copy if t % 2 == 0 else nc.scalar.copy, parts=1 if t < 10 else 2)
